import numpy as np
import ml_dtypes


def mxq(x, axis, fmt="e4m3"):
    dtype, down = {"e4m3": (ml_dtypes.float8_e4m3fn, 7), "e5m2": (ml_dtypes.float8_e5m2, 14)}[fmt]
    v = np.moveaxis(np.asarray(x, np.float32).astype(ml_dtypes.bfloat16).astype(np.float64), axis, -1)
    blocks = v.reshape(v.shape[:-1] + (-1, 32))
    amax = np.abs(blocks).max(-1, keepdims=True)
    byte = np.maximum(np.where(amax > 0, np.frexp(amax)[1] - 1 + 127, 0) - down, 1)
    scale = np.exp2(byte - 127.0)
    codes = (blocks / scale).astype(np.float32).astype(dtype).astype(np.float64)
    return np.moveaxis((codes * scale).reshape(v.shape), -1, axis)


WIDE = False


def mx_kscale(k):
    if not WIDE:
        return np.ones(k)
    levels = np.array([10, -10, 5, -5, 0])
    if k % 512:
        return np.exp2(np.random.permutation(np.resize(levels, k // 32))).repeat(32)
    a = np.empty((k // 512, 16))
    for p in range(k // 512):
        a[p, :8] = np.random.permutation(np.resize(levels, 8))
        for g in range(8):
            far = levels[np.abs(levels - a[p, g]) >= 10]
            a[p, g + 8] = far[np.random.randint(len(far))]
    return np.exp2(a.ravel()).repeat(32)


BF16 = ml_dtypes.bfloat16


def bf(x):
    return np.asarray(x, np.float32).astype(BF16)


def f64(x):
    return np.asarray(x).astype(np.float64)


N, N_CH, X, H = 4096, 4, 512, 256
K = N_CH * H
G = 3 * H


def sigmoid(v):
    return 1.0 / (1.0 + np.exp(-v))


def setup_inputs():
    s, t = mx_kscale(X), mx_kscale(K)
    return {
        "x": bf(np.random.standard_normal((N, X)) * s),
        "x_mask": bf(np.random.random(N) < 0.75),
        "neighbour_h": bf(np.random.standard_normal((N, N_CH, H)) * t.reshape(N_CH, H)),
        "c_aggr": bf(np.random.standard_normal((N, H)) * 0.57 * np.sqrt(N_CH)),
        "W_iou_in": bf(np.random.standard_normal((X, G)) / np.sqrt(X) / s[:, None]),
        "b_iou_in": bf(np.random.standard_normal(G) * 0.3),
        "W_aggr_iou": bf(np.random.standard_normal((K, G)) / np.sqrt(K) / t[:, None]),
        "b_aggr_iou": bf(np.random.standard_normal(G) * 0.3),
    }


def reference(x, x_mask, neighbour_h, c_aggr, W_iou_in, b_iou_in, W_aggr_iou, b_aggr_iou):
    h_flat = f64(neighbour_h).reshape(N, K)
    iou_aggr = (mxq(h_flat, 1, "e4m3") @ mxq(f64(W_aggr_iou), 0, "e4m3")) + f64(b_aggr_iou)
    iou = ((mxq(f64(x), 1, "e4m3") @ mxq(f64(W_iou_in), 0, "e4m3")) + f64(b_iou_in)) * f64(x_mask)[:, None] + iou_aggr
    i, o, u = np.split(iou, 3, axis=1)
    i, o, u = sigmoid(i), sigmoid(o), np.tanh(u)
    c = i * u + f64(c_aggr)
    h = o * np.tanh(c)
    return h, c

@@ -1,0 +1,299 @@
+from contextlib import ExitStack
+
+import concourse.mybir as mybir
+from concourse.masks import make_identity
+
+BF16 = mybir.dt.bfloat16
+F32 = mybir.dt.float32
+U32 = mybir.dt.uint32
+U8 = mybir.dt.uint8
+FP8X4 = mybir.dt.float8_e4m3fn_x4
+ACT = mybir.ActivationFunctionType
+ALU = mybir.AluOpType
+
+P = 128
+PACK = 4
+K_PASS = P * PACK
+NODES, X_DIM, CHILDREN, H_DIM = 4096, 512, 4, 256
+HF_DIM = CHILDREN * H_DIM
+GATES = 3 * H_DIM
+PASSES = (X_DIM + HF_DIM) // K_PASS
+GATE_TILES = GATES // P
+H_TILES = H_DIM // P
+NODE_TILES = NODES // P
+CHUNK = 512
+CHUNK_TILES = CHUNK // P
+CHUNKS = NODES // CHUNK
+WORDS = P
+BANK_TILES = 2
+HALVES = CHUNK_TILES // BANK_TILES
+I_TILES, O_TILES, U_TILES = (0, 1), (2, 3), (4, 5)
+
+FLOPS = 2 * NODES * (X_DIM + HF_DIM) * GATES
+
+
+def tile_treelstmcell_pb_t_kernel(
+    tc, x, x_mask, neighbour_h, c_aggr, W_iou_in, b_iou_in, W_aggr_iou, b_aggr_iou, out_0, out_1
+):
+    nc = tc.nc
+
+    x_rows = x.rearrange("(p t) k -> p (t k)", t=NODE_TILES)
+    hf_rows = neighbour_h.rearrange("(p t) c f -> p (t c f)", t=NODE_TILES)
+    c_aggr_rows = c_aggr.rearrange("(p t) f -> p t f", t=NODE_TILES)
+    h_rows = out_0.rearrange("(p t) f -> p t f", t=NODE_TILES)
+    c_rows = out_1.rearrange("(p t) f -> p t f", t=NODE_TILES)
+
+    with ExitStack() as ctx:
+        const = ctx.enter_context(tc.tile_pool(name="const", bufs=1))
+        wstage = ctx.enter_context(tc.tile_pool(name="wstage", bufs=3))
+        loads = ctx.enter_context(tc.tile_pool(name="loads", bufs=3))
+        acts = ctx.enter_context(tc.tile_pool(name="acts", bufs=2))
+        work = ctx.enter_context(tc.tile_pool(name="work", bufs=2))
+        psum_tp = ctx.enter_context(tc.psum_pool(name="psum_tp", bufs=3))
+        psum_z = ctx.enter_context(tc.psum_pool(name="psum_z", bufs=3))
+        psum_bt = ctx.enter_context(tc.psum_pool(name="psum_bt", bufs=2))
+
+        ctx.enter_context(tc.manual_schedule())
+
+        x_sb, hf_sb, c_aggr_sb = {}, {}, {}
+        w_raw, w_grouped = {}, {}
+        a_grouped, a_codes, a_scales = {}, {}, {}
+        gates, i_times_u, c_new, tanh_c = {}, {}, {}, {}
+
+        ident = const.tile([P, P], F32)
+        make_identity(nc, ident[:])
+        ident_bf = const.tile([P, P], BF16)
+        make_identity(nc, ident_bf[:])
+
+        mask_col = const.tile([P, NODE_TILES], BF16)
+        nc.sync.dma_start(out=mask_col[:], in_=x_mask.rearrange("(p t) -> p t", t=NODE_TILES))
+        mask_f32 = const.tile([P, NODE_TILES], F32)
+        mask_row = const.tile([P, NODE_TILES, P], BF16)
+
+        diag = const.tile([P, NODE_TILES, P], F32)
+
+        def load(c):
+            x_sb[c] = loads.tile([P, CHUNK_TILES * X_DIM], BF16, name="x_sb")
+            nc.sync.dma_start(out=x_sb[c][:], in_=x_rows[:, c * CHUNK_TILES * X_DIM : (c + 1) * CHUNK_TILES * X_DIM])
+            hf_sb[c] = loads.tile([P, CHUNK_TILES * HF_DIM], BF16, name="hf_sb")
+            nc.sync.dma_start(
+                out=hf_sb[c][:], in_=hf_rows[:, c * CHUNK_TILES * HF_DIM : (c + 1) * CHUNK_TILES * HF_DIM]
+            )
+
+        def load_c_aggr(c):
+            c_aggr_sb[c] = loads.tile([P, CHUNK_TILES, H_DIM], BF16, name="c_aggr_sb")
+            nc.sync.dma_start(out=c_aggr_sb[c][:], in_=c_aggr_rows[:, c * CHUNK_TILES : (c + 1) * CHUNK_TILES, :])
+
+        def mask_identity(c):
+            tiles = slice(c * CHUNK_TILES, (c + 1) * CHUNK_TILES)
+            nc.gpsimd.tensor_tensor(
+                out=diag[:, tiles, :],
+                in0=ident[:].unsqueeze(1).to_broadcast([P, CHUNK_TILES, P]),
+                in1=mask_col[:, tiles].unsqueeze(2).to_broadcast([P, CHUNK_TILES, P]),
+                op=ALU.mult,
+            )
+
+        def spread_mask(c):
+            spread = psum_z.tile([P, CHUNK_TILES, P], F32, name="spread", tag="sums")
+            for j in range(CHUNK_TILES):
+                t = c * CHUNK_TILES + j
+                nc.tensor.transpose(spread[:, j, :], mask_f32[:, t : t + 1].to_broadcast([P, P]), ident[:])
+            nc.scalar.copy(out=mask_row[:, c * CHUNK_TILES : (c + 1) * CHUNK_TILES, :], in_=spread[:])
+
+        def transpose_in(c, g):
+            if c not in a_grouped:
+                a_grouped[c] = acts.tile([P, PASSES * CHUNK * PACK], BF16, name="a_grouped", align_bytes=64)
+            if g == 0:
+                words, tile_words, first_word = x_sb[c][:].bitcast(F32), X_DIM // 2, 0
+            else:
+                words, tile_words, first_word = hf_sb[c][:].bitcast(F32), HF_DIM // 2, (g - 1) * (K_PASS // 2)
+            grouped_words = a_grouped[c][:].bitcast(F32)
+            for half in range(HALVES):
+                kT = psum_tp.tile([P, 2, BANK_TILES * P], F32, name="kT")
+                for jj in range(BANK_TILES):
+                    j = half * BANK_TILES + jj
+                    for u in range(2):
+                        first = j * tile_words + first_word
+                        perm = diag[:, c * CHUNK_TILES + j, :] if g == 0 else ident[:]
+                        nc.tensor.transpose(
+                            kT[:, u, jj * P : (jj + 1) * P], words[:, first + u : first + 2 * WORDS : 2], perm
+                        )
+                first = (g * CHUNK + half * BANK_TILES * P) * 2
+                nc.scalar.copy(
+                    out=grouped_words[:, first : first + BANK_TILES * P * 2].rearrange("p (n u) -> p n u", u=2),
+                    in_=kT[:].rearrange("p u n -> p n u"),
+                )
+
+        def quantise(c, g):
+            if c not in a_codes:
+                a_codes[c] = acts.tile([P, PASSES * CHUNK], U32, name="a_codes", align_bytes=64)
+                a_scales[c] = acts.tile([P, PASSES * CHUNK], U8, name="a_scales", align_bytes=64)
+            cols = slice(g * CHUNK, (g + 1) * CHUNK)
+            nc.vector.quantize_mx(
+                out=a_codes[c][:, cols].bitcast(FP8X4),
+                scales=a_scales[c][:, cols],
+                in_=a_grouped[c][:, g * CHUNK * PACK : (g + 1) * CHUNK * PACK],
+            )
+
+        def gate_tiles(c, some):
+            if c not in gates:
+                gates[c] = work.tile([P, GATE_TILES, CHUNK], F32, name="gates")
+            for m in some:
+                sums = psum_z.tile([P, CHUNK], F32, name="sums")
+                for g in range(PASSES):
+                    w_cols = slice(g * GATES + m * P, g * GATES + (m + 1) * P)
+                    a_cols = slice(g * CHUNK, (g + 1) * CHUNK)
+                    nc.tensor.matmul_mx(
+                        out=sums[:],
+                        lhsT=w_codes[:, w_cols].bitcast(FP8X4),
+                        lhsT_scale=w_scales[:, w_cols],
+                        rhs=a_codes[c][:, a_cols].bitcast(FP8X4),
+                        rhs_scale=a_scales[c][:, a_cols],
+                        start=(g == 0),
+                        stop=(g == PASSES - 1),
+                    )
+                masked = work.tile([P, CHUNK], F32, name="masked", bufs=4)
+                nc.vector.scalar_tensor_tensor(
+                    out=masked[:],
+                    in0=mask_row[:, c * CHUNK_TILES : (c + 1) * CHUNK_TILES, :].rearrange("q t p -> q (t p)"),
+                    scalar=bias_col[:, m : m + 1],
+                    in1=sums[:],
+                    op0=ALU.mult,
+                    op1=ALU.add,
+                )
+                nc.scalar.activation(
+                    out=gates[c][:, m, :],
+                    in_=masked[:],
+                    func=(ACT.Tanh if m in U_TILES else ACT.Sigmoid),
+                    bias=bias_col[:, GATE_TILES + m : GATE_TILES + m + 1],
+                    scale=1.0,
+                )
+
+        def multiply_i_u(c):
+            i_times_u[c] = work.tile([P, H_TILES, CHUNK], F32, name="i_times_u")
+            for half in range(HALVES):
+                cols = slice(half * BANK_TILES * P, (half + 1) * BANK_TILES * P)
+                nc.gpsimd.tensor_tensor(
+                    out=i_times_u[c][:, :, cols],
+                    in0=gates[c][:, I_TILES[0] : I_TILES[0] + H_TILES, cols],
+                    in1=gates[c][:, U_TILES[0] : U_TILES[0] + H_TILES, cols],
+                    op=ALU.mult,
+                )
+
+        def transpose_back(source, first_tile, half):
+            back = psum_bt.tile([P, BANK_TILES, H_DIM], F32, name="back")
+            for jj in range(BANK_TILES):
+                j = half * BANK_TILES + jj
+                for f in range(H_TILES):
+                    nc.tensor.transpose(
+                        back[:, jj, f * P : (f + 1) * P], source[:, first_tile + f, j * P : (j + 1) * P], ident[:]
+                    )
+            return back
+
+        def cell_state(c):
+            c_new[c] = work.tile([P, CHUNK_TILES, H_DIM], F32, name="c_new", bufs=3)
+            tanh_c[c] = work.tile([P, CHUNK_TILES, H_DIM], F32, name="tanh_c")
+            for half in range(HALVES):
+                tiles = slice(half * BANK_TILES, (half + 1) * BANK_TILES)
+                back = transpose_back(i_times_u[c], 0, half)
+                nc.vector.tensor_tensor(out=c_new[c][:, tiles, :], in0=back[:], in1=c_aggr_sb[c][:, tiles, :], op=ALU.add)
+                nc.scalar.activation(out=tanh_c[c][:, tiles, :], in_=c_new[c][:, tiles, :], func=ACT.Tanh)
+                first = c * CHUNK_TILES + half * BANK_TILES
+                nc.sync.dma_start(out=c_rows[:, first : first + BANK_TILES, :], in_=c_new[c][:, tiles, :])
+
+        def hidden_state(c):
+            h_new = work.tile([P, CHUNK_TILES, H_DIM], F32, name="h_new", bufs=3)
+            for half in range(HALVES):
+                tiles = slice(half * BANK_TILES, (half + 1) * BANK_TILES)
+                back = transpose_back(gates[c], O_TILES[0], half)
+                nc.vector.tensor_tensor(out=h_new[:, tiles, :], in0=back[:], in1=tanh_c[c][:, tiles, :], op=ALU.mult)
+                first = c * CHUNK_TILES + half * BANK_TILES
+                nc.sync.dma_start(out=h_rows[:, first : first + BANK_TILES, :], in_=h_new[:, tiles, :])
+
+        w_codes = const.tile([P, PASSES * GATES], U32, align_bytes=64)
+        w_scales = const.tile([P, PASSES * GATES], U8, align_bytes=64)
+
+        def load_weights(g):
+            rows = W_iou_in if g == 0 else W_aggr_iou[(g - 1) * K_PASS : g * K_PASS, :]
+            w_raw[g] = wstage.tile([P, PACK, GATES], BF16, name="w_raw")
+            nc.sync.dma_start(
+                out=w_raw[g][:].rearrange("q t c -> q (t c)"),
+                in_=rows.rearrange("(q t) c -> q (t c)", t=PACK),
+            )
+
+        def group_weights(g):
+            w_grouped[g] = wstage.tile([P, GATES, PACK], BF16, name="w_grouped", align_bytes=64, bufs=2)
+            nc.vector.tensor_copy(out=w_grouped[g][:], in_=w_raw[g][:].rearrange("q t c -> q c t"))
+
+        def quantise_weights(g):
+            for first, cols in ((0, 512), (512, 256)):
+                nc.vector.quantize_mx(
+                    out=w_codes[:, g * GATES + first : g * GATES + first + cols].bitcast(FP8X4),
+                    scales=w_scales[:, g * GATES + first : g * GATES + first + cols],
+                    in_=w_grouped[g][:].rearrange("q c t -> q (c t)")[:, first * PACK : (first + cols) * PACK],
+                )
+
+        bias_rows = const.tile([P, P], BF16)
+        nc.vector.memset(bias_rows[:], 0.0)
+        nc.vector.tensor_copy(out=mask_f32[:], in_=mask_col[:])
+        for g in range(PASSES):
+            load_weights(g)
+        load(0)
+        nc.sync.dma_start(out=bias_rows[0:GATE_TILES, :], in_=b_iou_in.rearrange("(m g) -> m g", g=P))
+        nc.sync.dma_start(out=bias_rows[GATE_TILES : 2 * GATE_TILES, :], in_=b_aggr_iou.rearrange("(m g) -> m g", g=P))
+        load(1)
+        load(2)
+        load_c_aggr(0)
+        mask_identity(0)
+        mask_identity(1)
+        for c in range(CHUNKS):
+            spread_mask(c)
+
+        group_weights(0)
+        for g in range(1, PASSES):
+            group_weights(g)
+            quantise_weights(g - 1)
+        quantise_weights(PASSES - 1)
+
+        for g in range(PASSES):
+            transpose_in(0, g)
+        for g in range(PASSES):
+            quantise(0, g)
+        transpose_in(1, 0)
+
+        bias_ps = psum_bt.tile([P, P], BF16, name="bias_ps", tag="back")
+        nc.tensor.transpose(bias_ps[:], bias_rows[:], ident_bf[:])
+        bias_col = const.tile([P, 2 * GATE_TILES], F32)
+        nc.vector.tensor_copy(out=bias_col[:], in_=bias_ps[:, 0 : 2 * GATE_TILES])
+
+        for c in range(CHUNKS + 1):
+            if c + 3 < CHUNKS:
+                load(c + 3)
+            if c + 1 < CHUNKS:
+                load_c_aggr(c + 1)
+            if c + 2 < CHUNKS:
+                mask_identity(c + 2)
+
+            if c + 1 < CHUNKS:
+                transpose_in(c + 1, 1)
+            if c < CHUNKS:
+                gate_tiles(c, I_TILES)
+
+            if 0 <= c - 1:
+                cell_state(c - 1)
+            if c + 1 < CHUNKS:
+                transpose_in(c + 1, 2)
+                quantise(c + 1, 0)
+                quantise(c + 1, 1)
+            if c < CHUNKS:
+                gate_tiles(c, U_TILES)
+                multiply_i_u(c)
+            if c + 1 < CHUNKS:
+                quantise(c + 1, 2)
+
+            if 0 <= c - 1:
+                hidden_state(c - 1)
+            if c + 2 < CHUNKS:
+                transpose_in(c + 2, 0)
+            if c < CHUNKS:
+                gate_tiles(c, O_TILES)

@@ -26,9 +26,14 @@ CHUNK_TILES = CHUNK // P
 CHUNKS = NODES // CHUNK
 WORDS = P
 BANK_TILES = 2
+SPREAD_TILES = 8
 HALVES = CHUNK_TILES // BANK_TILES
 I_TILES, O_TILES, U_TILES = (0, 1), (2, 3), (4, 5)
+W_PARTS = ((0, H_DIM), (H_DIM, 2 * H_DIM))
 
+XMODE = "g"
+XSTRIDED = ()
+HSTRIDED = ((0, 1), (0, 2), (1, 1), (1, 2))
 FLOPS = 2 * NODES * (X_DIM + HF_DIM) * GATES
 
 
@@ -47,15 +52,15 @@ def tile_treelstmcell_pb_t_kernel(
         const = ctx.enter_context(tc.tile_pool(name="const", bufs=1))
         wstage = ctx.enter_context(tc.tile_pool(name="wstage", bufs=3))
         loads = ctx.enter_context(tc.tile_pool(name="loads", bufs=3))
+        ordered = ctx.enter_context(tc.tile_pool(name="ordered", bufs=2))
         acts = ctx.enter_context(tc.tile_pool(name="acts", bufs=2))
         work = ctx.enter_context(tc.tile_pool(name="work", bufs=2))
-        psum_tp = ctx.enter_context(tc.psum_pool(name="psum_tp", bufs=3))
-        psum_z = ctx.enter_context(tc.psum_pool(name="psum_z", bufs=3))
-        psum_bt = ctx.enter_context(tc.psum_pool(name="psum_bt", bufs=2))
+        psum = ctx.enter_context(tc.psum_pool(name="psum", bufs=8))
 
         ctx.enter_context(tc.manual_schedule())
 
         x_sb, hf_sb, c_aggr_sb = {}, {}, {}
+        x_ordered, hf_ordered, diag = {}, {}, {}
         w_raw, w_grouped = {}, {}
         a_grouped, a_codes, a_scales = {}, {}, {}
         gates, i_times_u, c_new, tanh_c = {}, {}, {}, {}
@@ -70,11 +75,11 @@ def tile_treelstmcell_pb_t_kernel(
         mask_f32 = const.tile([P, NODE_TILES], F32)
         mask_row = const.tile([P, NODE_TILES, P], BF16)
 
-        diag = const.tile([P, NODE_TILES, P], F32)
-
-        def load(c):
-            x_sb[c] = loads.tile([P, CHUNK_TILES * X_DIM], BF16, name="x_sb")
+        def load_x(c):
+            x_sb[c] = loads.tile([P, CHUNK_TILES * X_DIM], BF16, name="x_sb", bufs=4)
             nc.sync.dma_start(out=x_sb[c][:], in_=x_rows[:, c * CHUNK_TILES * X_DIM : (c + 1) * CHUNK_TILES * X_DIM])
+
+        def load_hf(c):
             hf_sb[c] = loads.tile([P, CHUNK_TILES * HF_DIM], BF16, name="hf_sb")
             nc.sync.dma_start(
                 out=hf_sb[c][:], in_=hf_rows[:, c * CHUNK_TILES * HF_DIM : (c + 1) * CHUNK_TILES * HF_DIM]
@@ -84,40 +89,70 @@ def tile_treelstmcell_pb_t_kernel(
             c_aggr_sb[c] = loads.tile([P, CHUNK_TILES, H_DIM], BF16, name="c_aggr_sb")
             nc.sync.dma_start(out=c_aggr_sb[c][:], in_=c_aggr_rows[:, c * CHUNK_TILES : (c + 1) * CHUNK_TILES, :])
 
-        def mask_identity(c):
-            tiles = slice(c * CHUNK_TILES, (c + 1) * CHUNK_TILES)
-            nc.gpsimd.tensor_tensor(
-                out=diag[:, tiles, :],
-                in0=ident[:].unsqueeze(1).to_broadcast([P, CHUNK_TILES, P]),
-                in1=mask_col[:, tiles].unsqueeze(2).to_broadcast([P, CHUNK_TILES, P]),
-                op=ALU.mult,
-            )
-
-        def spread_mask(c):
-            spread = psum_z.tile([P, CHUNK_TILES, P], F32, name="spread", tag="sums")
+        def mask_x(c):
+            if XMODE == "diag" or c in XSTRIDED:
+                diag[c] = ordered.tile([P, CHUNK_TILES, P], F32, name="diag")
+                nc.gpsimd.tensor_tensor(
+                    out=diag[c][:],
+                    in0=ident[:].unsqueeze(1).to_broadcast([P, CHUNK_TILES, P]),
+                    in1=mask_col[:, c * CHUNK_TILES : (c + 1) * CHUNK_TILES].unsqueeze(2).to_broadcast([P, CHUNK_TILES, P]),
+                    op=ALU.mult,
+                )
+                return
+            x_ordered[c] = ordered.tile([P, CHUNK_TILES, 2, WORDS, 2], BF16, name="x_ordered", bufs=3)
             for j in range(CHUNK_TILES):
                 t = c * CHUNK_TILES + j
-                nc.tensor.transpose(spread[:, j, :], mask_f32[:, t : t + 1].to_broadcast([P, P]), ident[:])
-            nc.scalar.copy(out=mask_row[:, c * CHUNK_TILES : (c + 1) * CHUNK_TILES, :], in_=spread[:])
+                eng = nc.gpsimd if XMODE == "g" else nc.vector
+                eng.tensor_scalar(
+                    out=x_ordered[c][:, j, :, :, :],
+                    in0=x_sb[c][:, j * X_DIM : (j + 1) * X_DIM].rearrange("p (w u e) -> p u w e", u=2, e=2),
+                    scalar1=mask_f32[:, t : t + 1],
+                    scalar2=0.0,
+                    op0=ALU.mult,
+                    op1=ALU.add,
+                )
+
+        def order_hf(c, g):
+            if (c, g) in HSTRIDED:
+                return
+            if c not in hf_ordered:
+                hf_ordered[c] = ordered.tile([P, PASSES - 1, CHUNK_TILES, 2, WORDS], F32, name="hf_ordered")
+            words = hf_sb[c][:].bitcast(F32).rearrange("p (j h w u) -> p h j u w", h=PASSES - 1, w=WORDS, u=2)
+            nc.vector.tensor_copy(out=hf_ordered[c][:, g - 1, :, :, :], in_=words[:, g - 1, :, :, :])
+
+        def spread_mask(first_tile):
+            spread = psum.tile([P, SPREAD_TILES, P], BF16, name="spread", tag="bank")
+            for j in range(SPREAD_TILES):
+                t = first_tile + j
+                nc.tensor.transpose(spread[:, j, :], mask_col[:, t : t + 1].to_broadcast([P, P]), ident_bf[:])
+            nc.scalar.copy(out=mask_row[:, first_tile : first_tile + SPREAD_TILES, :], in_=spread[:])
 
         def transpose_in(c, g):
             if c not in a_grouped:
                 a_grouped[c] = acts.tile([P, PASSES * CHUNK * PACK], BF16, name="a_grouped", align_bytes=64)
-            if g == 0:
-                words, tile_words, first_word = x_sb[c][:].bitcast(F32), X_DIM // 2, 0
+            perm = lambda j: ident[:]
+            if g == 0 and c in diag:
+                sw = x_sb[c][:].bitcast(F32)
+                words = lambda j, u: sw[:, j * (X_DIM // 2) + u : (j + 1) * (X_DIM // 2) : 2]
+                perm = lambda j: diag[c][:, j, :]
+            elif g == 0:
+                x_words = x_ordered[c][:].rearrange("p j u w e -> p (j u w e)").bitcast(F32)
+                words = lambda j, u: x_words[:, (2 * j + u) * WORDS : (2 * j + u + 1) * WORDS]
+            elif (c, g) not in HSTRIDED:
+                words = lambda j, u: hf_ordered[c][:, g - 1, j, u, :]
             else:
-                words, tile_words, first_word = hf_sb[c][:].bitcast(F32), HF_DIM // 2, (g - 1) * (K_PASS // 2)
+                hf_words = hf_sb[c][:].bitcast(F32)
+                first_word = (g - 1) * (K_PASS // 2)
+                words = lambda j, u: hf_words[
+                    :, j * (HF_DIM // 2) + first_word + u : j * (HF_DIM // 2) + first_word + K_PASS // 2 : 2
+                ]
             grouped_words = a_grouped[c][:].bitcast(F32)
             for half in range(HALVES):
-                kT = psum_tp.tile([P, 2, BANK_TILES * P], F32, name="kT")
+                kT = psum.tile([P, 2, BANK_TILES * P], F32, name="kT", tag="bank")
                 for jj in range(BANK_TILES):
                     j = half * BANK_TILES + jj
                     for u in range(2):
-                        first = j * tile_words + first_word
-                        perm = diag[:, c * CHUNK_TILES + j, :] if g == 0 else ident[:]
-                        nc.tensor.transpose(
-                            kT[:, u, jj * P : (jj + 1) * P], words[:, first + u : first + 2 * WORDS : 2], perm
-                        )
+                        nc.tensor.transpose(kT[:, u, jj * P : (jj + 1) * P], words(j, u), perm(j))
                 first = (g * CHUNK + half * BANK_TILES * P) * 2
                 nc.scalar.copy(
                     out=grouped_words[:, first : first + BANK_TILES * P * 2].rearrange("p (n u) -> p n u", u=2),
@@ -135,29 +170,35 @@ def tile_treelstmcell_pb_t_kernel(
                 in_=a_grouped[c][:, g * CHUNK * PACK : (g + 1) * CHUNK * PACK],
             )
 
-        def gate_tiles(c, some):
+        def gate_tiles(c, some, pass_by_pass=False):
             if c not in gates:
                 gates[c] = work.tile([P, GATE_TILES, CHUNK], F32, name="gates")
+            sums = {}
             for m in some:
-                sums = psum_z.tile([P, CHUNK], F32, name="sums")
-                for g in range(PASSES):
-                    w_cols = slice(g * GATES + m * P, g * GATES + (m + 1) * P)
-                    a_cols = slice(g * CHUNK, (g + 1) * CHUNK)
-                    nc.tensor.matmul_mx(
-                        out=sums[:],
-                        lhsT=w_codes[:, w_cols].bitcast(FP8X4),
-                        lhsT_scale=w_scales[:, w_cols],
-                        rhs=a_codes[c][:, a_cols].bitcast(FP8X4),
-                        rhs_scale=a_scales[c][:, a_cols],
-                        start=(g == 0),
-                        stop=(g == PASSES - 1),
-                    )
+                sums[m] = psum.tile([P, CHUNK], F32, name="sums", tag="bank")
+            if pass_by_pass:
+                order = [(m, g) for g in range(PASSES) for m in some]
+            else:
+                order = [(m, g) for m in some for g in range(PASSES)]
+            for m, g in order:
+                w_cols = slice(g * GATES + m * P, g * GATES + (m + 1) * P)
+                a_cols = slice(g * CHUNK, (g + 1) * CHUNK)
+                nc.tensor.matmul_mx(
+                    out=sums[m][:],
+                    lhsT=w_codes[:, w_cols].bitcast(FP8X4),
+                    lhsT_scale=w_scales[:, w_cols],
+                    rhs=a_codes[c][:, a_cols].bitcast(FP8X4),
+                    rhs_scale=a_scales[c][:, a_cols],
+                    start=(g == 0),
+                    stop=(g == PASSES - 1),
+                )
+            for m in some:
                 masked = work.tile([P, CHUNK], F32, name="masked", bufs=4)
                 nc.vector.scalar_tensor_tensor(
                     out=masked[:],
                     in0=mask_row[:, c * CHUNK_TILES : (c + 1) * CHUNK_TILES, :].rearrange("q t p -> q (t p)"),
                     scalar=bias_col[:, m : m + 1],
-                    in1=sums[:],
+                    in1=sums[m][:],
                     op0=ALU.mult,
                     op1=ALU.add,
                 )
@@ -181,7 +222,7 @@ def tile_treelstmcell_pb_t_kernel(
                 )
 
         def transpose_back(source, first_tile, half):
-            back = psum_bt.tile([P, BANK_TILES, H_DIM], F32, name="back")
+            back = psum.tile([P, BANK_TILES, H_DIM], F32, name="back", tag="bank")
             for jj in range(BANK_TILES):
                 j = half * BANK_TILES + jj
                 for f in range(H_TILES):
@@ -191,7 +232,7 @@ def tile_treelstmcell_pb_t_kernel(
             return back
 
         def cell_state(c):
-            c_new[c] = work.tile([P, CHUNK_TILES, H_DIM], F32, name="c_new", bufs=3)
+            c_new[c] = work.tile([P, CHUNK_TILES, H_DIM], F32, name="c_new")
             tanh_c[c] = work.tile([P, CHUNK_TILES, H_DIM], F32, name="tanh_c")
             for half in range(HALVES):
                 tiles = slice(half * BANK_TILES, (half + 1) * BANK_TILES)
@@ -202,7 +243,7 @@ def tile_treelstmcell_pb_t_kernel(
                 nc.sync.dma_start(out=c_rows[:, first : first + BANK_TILES, :], in_=c_new[c][:, tiles, :])
 
         def hidden_state(c):
-            h_new = work.tile([P, CHUNK_TILES, H_DIM], F32, name="h_new", bufs=3)
+            h_new = work.tile([P, CHUNK_TILES, H_DIM], F32, name="h_new")
             for half in range(HALVES):
                 tiles = slice(half * BANK_TILES, (half + 1) * BANK_TILES)
                 back = transpose_back(gates[c], O_TILES[0], half)
@@ -221,62 +262,89 @@ def tile_treelstmcell_pb_t_kernel(
                 in_=rows.rearrange("(q t) c -> q (t c)", t=PACK),
             )
 
-        def group_weights(g):
-            w_grouped[g] = wstage.tile([P, GATES, PACK], BF16, name="w_grouped", align_bytes=64, bufs=2)
-            nc.vector.tensor_copy(out=w_grouped[g][:], in_=w_raw[g][:].rearrange("q t c -> q c t"))
+        def group_weights(g, part):
+            if g not in w_grouped:
+                w_grouped[g] = wstage.tile([P, GATES, PACK], BF16, name="w_grouped", align_bytes=64, bufs=2)
+            first, cols = part
+            nc.vector.tensor_copy(
+                out=w_grouped[g][:, first : first + cols, :],
+                in_=w_raw[g][:, :, first : first + cols].rearrange("q t c -> q c t"),
+            )
 
-        def quantise_weights(g):
-            for first, cols in ((0, 512), (512, 256)):
-                nc.vector.quantize_mx(
-                    out=w_codes[:, g * GATES + first : g * GATES + first + cols].bitcast(FP8X4),
-                    scales=w_scales[:, g * GATES + first : g * GATES + first + cols],
-                    in_=w_grouped[g][:].rearrange("q c t -> q (c t)")[:, first * PACK : (first + cols) * PACK],
-                )
+        def quantise_weights(g, part):
+            first, cols = part
+            nc.vector.quantize_mx(
+                out=w_codes[:, g * GATES + first : g * GATES + first + cols].bitcast(FP8X4),
+                scales=w_scales[:, g * GATES + first : g * GATES + first + cols],
+                in_=w_grouped[g][:].rearrange("q c t -> q (c t)")[:, first * PACK : (first + cols) * PACK],
+            )
 
         bias_rows = const.tile([P, P], BF16)
         nc.vector.memset(bias_rows[:], 0.0)
+        warm = const.tile([P, 1], BF16)
+        nc.scalar.activation(out=warm[:], in_=bias_rows[:, 0:1], func=ACT.Sigmoid)
         nc.vector.tensor_copy(out=mask_f32[:], in_=mask_col[:])
-        for g in range(PASSES):
-            load_weights(g)
-        load(0)
+        load_weights(0)
+        load_x(0)
+        load_weights(1)
+        load_hf(0)
         nc.sync.dma_start(out=bias_rows[0:GATE_TILES, :], in_=b_iou_in.rearrange("(m g) -> m g", g=P))
         nc.sync.dma_start(out=bias_rows[GATE_TILES : 2 * GATE_TILES, :], in_=b_aggr_iou.rearrange("(m g) -> m g", g=P))
-        load(1)
-        load(2)
+        load_weights(2)
+        load_x(1)
+        load_hf(1)
         load_c_aggr(0)
-        mask_identity(0)
-        mask_identity(1)
-        for c in range(CHUNKS):
-            spread_mask(c)
+        load_x(2)
+        load_hf(2)
+        if XMODE != "v":
+            mask_x(0)
+            mask_x(1)
+        for t in range(0, NODE_TILES, SPREAD_TILES):
+            spread_mask(t)
 
-        group_weights(0)
-        for g in range(1, PASSES):
-            group_weights(g)
-            quantise_weights(g - 1)
-        quantise_weights(PASSES - 1)
-
-        for g in range(PASSES):
-            transpose_in(0, g)
-        for g in range(PASSES):
-            quantise(0, g)
-        transpose_in(1, 0)
-
-        bias_ps = psum_bt.tile([P, P], BF16, name="bias_ps", tag="back")
+        for part in W_PARTS:
+            group_weights(0, part)
+        if XMODE == "v":
+            mask_x(0)
+        for part in W_PARTS:
+            quantise_weights(0, part)
+        transpose_in(0, 0)
+        for part in W_PARTS:
+            group_weights(1, part)
+        quantise(0, 0)
+        for part in W_PARTS:
+            quantise_weights(1, part)
+        transpose_in(0, 1)
+        transpose_in(0, 2)
+        bias_ps = psum.tile([P, P], BF16, name="bias_ps", tag="bank")
         nc.tensor.transpose(bias_ps[:], bias_rows[:], ident_bf[:])
         bias_col = const.tile([P, 2 * GATE_TILES], F32)
         nc.vector.tensor_copy(out=bias_col[:], in_=bias_ps[:, 0 : 2 * GATE_TILES])
+        quantise(0, 1)
+        group_weights(2, W_PARTS[0])
+        quantise(0, 2)
+        quantise_weights(2, W_PARTS[0])
+        group_weights(2, W_PARTS[1])
+        quantise_weights(2, W_PARTS[1])
+        gate_tiles(0, I_TILES, pass_by_pass=True)
+        if XMODE == "v":
+            mask_x(1)
+        transpose_in(1, 0)
 
         for c in range(CHUNKS + 1):
             if c + 3 < CHUNKS:
-                load(c + 3)
+                load_x(c + 3)
+                load_hf(c + 3)
             if c + 1 < CHUNKS:
                 load_c_aggr(c + 1)
             if c + 2 < CHUNKS:
-                mask_identity(c + 2)
+                mask_x(c + 2)
+            if c + 2 < CHUNKS:
+                order_hf(c + 2, 1)
 
             if c + 1 < CHUNKS:
                 transpose_in(c + 1, 1)
-            if c < CHUNKS:
+            if 0 < c < CHUNKS:
                 gate_tiles(c, I_TILES)
 
             if 0 <= c - 1:
@@ -285,6 +353,8 @@ def tile_treelstmcell_pb_t_kernel(
                 transpose_in(c + 1, 2)
                 quantise(c + 1, 0)
                 quantise(c + 1, 1)
+            if c + 2 < CHUNKS:
+                order_hf(c + 2, 2)
             if c < CHUNKS:
                 gate_tiles(c, U_TILES)
                 multiply_i_u(c)

@@ -31,7 +31,7 @@ HALVES = CHUNK_TILES // BANK_TILES
 I_TILES, O_TILES, U_TILES = (0, 1), (2, 3), (4, 5)
 W_PARTS = ((0, H_DIM), (H_DIM, 2 * H_DIM))
 
-XMODE = "g"
+XMODE = "sdiag"
 XSTRIDED = ()
 HSTRIDED = ((0, 1), (0, 2), (1, 1), (1, 2))
 FLOPS = 2 * NODES * (X_DIM + HF_DIM) * GATES
@@ -90,7 +90,13 @@ def tile_treelstmcell_pb_t_kernel(
             nc.sync.dma_start(out=c_aggr_sb[c][:], in_=c_aggr_rows[:, c * CHUNK_TILES : (c + 1) * CHUNK_TILES, :])
 
         def mask_x(c):
-            if XMODE == "diag" or c in XSTRIDED:
+            if XMODE == "sdiag" or c in XSTRIDED:
+                diag[c] = ordered.tile([P, CHUNK_TILES, P], F32, name="diag")
+                for j in range(CHUNK_TILES):
+                    t = c * CHUNK_TILES + j
+                    nc.scalar.activation(out=diag[c][:, j, :], in_=ident[:], func=ACT.Copy, scale=mask_f32[:, t : t + 1])
+                return
+            if XMODE == "diag":
                 diag[c] = ordered.tile([P, CHUNK_TILES, P], F32, name="diag")
                 nc.gpsimd.tensor_tensor(
                     out=diag[c][:],

@@ -29,11 +29,12 @@ BANK_TILES = 2
 SPREAD_TILES = 8
 HALVES = CHUNK_TILES // BANK_TILES
 I_TILES, O_TILES, U_TILES = (0, 1), (2, 3), (4, 5)
-W_PARTS = ((0, H_DIM), (H_DIM, 2 * H_DIM))
+I_PART, O_PART, U_PART = (0, H_DIM), (H_DIM, H_DIM), (2 * H_DIM, H_DIM)
+OU_PART = (H_DIM, 2 * H_DIM)
 
 XMODE = "sdiag"
 XSTRIDED = ()
-HSTRIDED = ((0, 1), (0, 2), (1, 1), (1, 2))
+HSTRIDED = ((0, 1), (0, 2), (1, 1), (1, 2), (2, 1), (2, 2), (3, 1), (3, 2), (4, 1), (4, 2), (5, 1), (5, 2), (6, 1), (6, 2), (7, 1), (7, 2))
 FLOPS = 2 * NODES * (X_DIM + HF_DIM) * GATES
 
 
@@ -63,7 +64,7 @@ def tile_treelstmcell_pb_t_kernel(
         x_ordered, hf_ordered, diag = {}, {}, {}
         w_raw, w_grouped = {}, {}
         a_grouped, a_codes, a_scales = {}, {}, {}
-        gates, i_times_u, c_new, tanh_c = {}, {}, {}, {}
+        gates, sums, i_times_u, c_new, tanh_c = {}, {}, {}, {}, {}
 
         ident = const.tile([P, P], F32)
         make_identity(nc, ident[:])
@@ -176,10 +177,9 @@ def tile_treelstmcell_pb_t_kernel(
                 in_=a_grouped[c][:, g * CHUNK * PACK : (g + 1) * CHUNK * PACK],
             )
 
-        def gate_tiles(c, some, pass_by_pass=False):
+        def gate_sums(c, some, pass_by_pass=False):
             if c not in gates:
                 gates[c] = work.tile([P, GATE_TILES, CHUNK], F32, name="gates")
-            sums = {}
             for m in some:
                 sums[m] = psum.tile([P, CHUNK], F32, name="sums", tag="bank")
             if pass_by_pass:
@@ -198,6 +198,7 @@ def tile_treelstmcell_pb_t_kernel(
                     start=(g == 0),
                     stop=(g == PASSES - 1),
                 )
+        def gate_exits(c, some):
             for m in some:
                 masked = work.tile([P, CHUNK], F32, name="masked", bufs=4)
                 nc.vector.scalar_tensor_tensor(
@@ -215,6 +216,10 @@ def tile_treelstmcell_pb_t_kernel(
                     bias=bias_col[:, GATE_TILES + m : GATE_TILES + m + 1],
                     scale=1.0,
                 )
+
+        def gate_tiles(c, some, pass_by_pass=False):
+            gate_sums(c, some, pass_by_pass)
+            gate_exits(c, some)
 
         def multiply_i_u(c):
             i_times_u[c] = work.tile([P, H_TILES, CHUNK], F32, name="i_times_u")
@@ -260,19 +265,21 @@ def tile_treelstmcell_pb_t_kernel(
         w_codes = const.tile([P, PASSES * GATES], U32, align_bytes=64)
         w_scales = const.tile([P, PASSES * GATES], U8, align_bytes=64)
 
-        def load_weights(g):
+        def load_weights(g, part):
             rows = W_iou_in if g == 0 else W_aggr_iou[(g - 1) * K_PASS : g * K_PASS, :]
-            w_raw[g] = wstage.tile([P, PACK, GATES], BF16, name="w_raw")
+            if g not in w_raw:
+                w_raw[g] = wstage.tile([P, PACK, GATES], BF16, name="w_raw")
+            first, cols = part
             nc.sync.dma_start(
-                out=w_raw[g][:].rearrange("q t c -> q (t c)"),
-                in_=rows.rearrange("(q t) c -> q (t c)", t=PACK),
+                out=w_raw[g][:, :, first : first + cols],
+                in_=rows[:, first : first + cols].rearrange("(q t) c -> q t c", t=PACK),
             )
 
-        def group_weights(g, part):
+        def group_weights(g, part, scalar=False):
             if g not in w_grouped:
-                w_grouped[g] = wstage.tile([P, GATES, PACK], BF16, name="w_grouped", align_bytes=64, bufs=2)
+                w_grouped[g] = wstage.tile([P, GATES, PACK], BF16, name="w_grouped", align_bytes=64)
             first, cols = part
-            nc.vector.tensor_copy(
+            (nc.scalar.copy if scalar else nc.vector.tensor_copy)(
                 out=w_grouped[g][:, first : first + cols, :],
                 in_=w_raw[g][:, :, first : first + cols].rearrange("q t c -> q c t"),
             )
@@ -290,52 +297,60 @@ def tile_treelstmcell_pb_t_kernel(
         warm = const.tile([P, 1], BF16)
         nc.scalar.activation(out=warm[:], in_=bias_rows[:, 0:1], func=ACT.Sigmoid)
         nc.vector.tensor_copy(out=mask_f32[:], in_=mask_col[:])
-        load_weights(0)
+        load_weights(0, I_PART)
         load_x(0)
-        load_weights(1)
+        load_weights(1, I_PART)
         load_hf(0)
         nc.sync.dma_start(out=bias_rows[0:GATE_TILES, :], in_=b_iou_in.rearrange("(m g) -> m g", g=P))
         nc.sync.dma_start(out=bias_rows[GATE_TILES : 2 * GATE_TILES, :], in_=b_aggr_iou.rearrange("(m g) -> m g", g=P))
-        load_weights(2)
+        load_weights(2, I_PART)
+        for g in range(PASSES):
+            load_weights(g, OU_PART)
         load_x(1)
         load_hf(1)
         load_c_aggr(0)
         load_x(2)
         load_hf(2)
-        if XMODE != "v":
-            mask_x(0)
-            mask_x(1)
+        mask_x(0)
+        mask_x(1)
         for t in range(0, NODE_TILES, SPREAD_TILES):
             spread_mask(t)
-
-        for part in W_PARTS:
-            group_weights(0, part)
-        if XMODE == "v":
-            mask_x(0)
-        for part in W_PARTS:
-            quantise_weights(0, part)
+        group_weights(0, I_PART)
         transpose_in(0, 0)
-        for part in W_PARTS:
-            group_weights(1, part)
+        group_weights(1, I_PART)
+        quantise_weights(0, I_PART)
         quantise(0, 0)
-        for part in W_PARTS:
-            quantise_weights(1, part)
+        quantise_weights(1, I_PART)
         transpose_in(0, 1)
         transpose_in(0, 2)
         bias_ps = psum.tile([P, P], BF16, name="bias_ps", tag="bank")
         nc.tensor.transpose(bias_ps[:], bias_rows[:], ident_bf[:])
         bias_col = const.tile([P, 2 * GATE_TILES], F32)
         nc.vector.tensor_copy(out=bias_col[:], in_=bias_ps[:, 0 : 2 * GATE_TILES])
+        group_weights(2, I_PART)
         quantise(0, 1)
-        group_weights(2, W_PARTS[0])
+        quantise_weights(2, I_PART)
         quantise(0, 2)
-        quantise_weights(2, W_PARTS[0])
-        group_weights(2, W_PARTS[1])
-        quantise_weights(2, W_PARTS[1])
-        gate_tiles(0, I_TILES, pass_by_pass=True)
-        if XMODE == "v":
-            mask_x(1)
+        gate_sums(0, I_TILES, True)
+        group_weights(0, O_PART, True)
+        group_weights(1, O_PART, True)
+        group_weights(2, O_PART, True)
+        group_weights(0, U_PART)
+        group_weights(1, U_PART)
+        quantise_weights(0, U_PART)
+        gate_exits(0, I_TILES)
+        group_weights(2, U_PART)
+        quantise_weights(1, U_PART)
+        quantise_weights(2, U_PART)
         transpose_in(1, 0)
+        gate_sums(0, U_TILES)
+        quantise_weights(0, O_PART)
+        gate_exits(0, U_TILES)
+        quantise_weights(1, O_PART)
+        quantise_weights(2, O_PART)
+        multiply_i_u(0)
+        quantise(1, 0)
+        transpose_in(1, 1)
 
         for c in range(CHUNKS + 1):
             if c + 3 < CHUNKS:
@@ -348,7 +363,7 @@ def tile_treelstmcell_pb_t_kernel(
             if c + 2 < CHUNKS:
                 order_hf(c + 2, 1)
 
-            if c + 1 < CHUNKS:
+            if 0 < c and c + 1 < CHUNKS:
                 transpose_in(c + 1, 1)
             if 0 < c < CHUNKS:
                 gate_tiles(c, I_TILES)
@@ -357,11 +372,12 @@ def tile_treelstmcell_pb_t_kernel(
                 cell_state(c - 1)
             if c + 1 < CHUNKS:
                 transpose_in(c + 1, 2)
-                quantise(c + 1, 0)
+                if c > 0:
+                    quantise(c + 1, 0)
                 quantise(c + 1, 1)
             if c + 2 < CHUNKS:
                 order_hf(c + 2, 2)
-            if c < CHUNKS:
+            if 0 < c < CHUNKS:
                 gate_tiles(c, U_TILES)
                 multiply_i_u(c)
             if c + 1 < CHUNKS:

@@ -23,15 +23,17 @@ H_TILES = H_DIM // P
 NODE_TILES = NODES // P
 CHUNK = 512
 CHUNK_TILES = CHUNK // P
-CHUNKS = NODES // CHUNK
+CHUNK_LIST = (4, 4, 4, 4, 4, 4, 4, 4)
+CHUNKS = len(CHUNK_LIST)
+FIRST_TILE = [sum(CHUNK_LIST[:c]) for c in range(CHUNKS)]
 WORDS = P
 BANK_TILES = 2
 SPREAD_TILES = 8
-HALVES = CHUNK_TILES // BANK_TILES
 I_TILES, O_TILES, U_TILES = (0, 1), (2, 3), (4, 5)
 I_PART, O_PART, U_PART = (0, H_DIM), (H_DIM, H_DIM), (2 * H_DIM, H_DIM)
 OU_PART = (H_DIM, 2 * H_DIM)
 
+IU_PIECES = 2
 XMODE = "sdiag"
 XSTRIDED = ()
 HSTRIDED = ((0, 1), (0, 2), (1, 1), (1, 2), (2, 1), (2, 2), (3, 1), (3, 2), (4, 1), (4, 2), (5, 1), (5, 2), (6, 1), (6, 2), (7, 1), (7, 2))
@@ -64,7 +66,7 @@ def tile_treelstmcell_pb_t_kernel(
         x_ordered, hf_ordered, diag = {}, {}, {}
         w_raw, w_grouped = {}, {}
         a_grouped, a_codes, a_scales = {}, {}, {}
-        gates, sums, i_times_u, c_new, tanh_c = {}, {}, {}, {}, {}
+        gates, sums, i_times_u, c_new, tanh_c, h_state = {}, {}, {}, {}, {}, {}
 
         ident = const.tile([P, P], F32)
         make_identity(nc, ident[:])
@@ -77,53 +79,65 @@ def tile_treelstmcell_pb_t_kernel(
         mask_row = const.tile([P, NODE_TILES, P], BF16)
 
         def load_x(c):
-            x_sb[c] = loads.tile([P, CHUNK_TILES * X_DIM], BF16, name="x_sb", bufs=4)
-            nc.sync.dma_start(out=x_sb[c][:], in_=x_rows[:, c * CHUNK_TILES * X_DIM : (c + 1) * CHUNK_TILES * X_DIM])
+            first, tiles = FIRST_TILE[c], CHUNK_LIST[c]
+            x_sb[c] = loads.tile([P, tiles * X_DIM], BF16, name="x_sb", bufs=4)
+            nc.sync.dma_start(out=x_sb[c][:], in_=x_rows[:, first * X_DIM : (first + tiles) * X_DIM])
 
         def load_hf(c):
-            hf_sb[c] = loads.tile([P, CHUNK_TILES * HF_DIM], BF16, name="hf_sb")
-            nc.sync.dma_start(
-                out=hf_sb[c][:], in_=hf_rows[:, c * CHUNK_TILES * HF_DIM : (c + 1) * CHUNK_TILES * HF_DIM]
-            )
+            first, tiles = FIRST_TILE[c], CHUNK_LIST[c]
+            hf_sb[c] = loads.tile([P, tiles * HF_DIM], BF16, name="hf_sb")
+            step = BANK_TILES if c == 0 else tiles
+            for j in range(0, tiles, step):
+                nc.sync.dma_start(
+                    out=hf_sb[c][:, j * HF_DIM : (j + step) * HF_DIM],
+                    in_=hf_rows[:, (first + j) * HF_DIM : (first + j + step) * HF_DIM],
+                )
 
         def load_c_aggr(c):
-            c_aggr_sb[c] = loads.tile([P, CHUNK_TILES, H_DIM], BF16, name="c_aggr_sb")
-            nc.sync.dma_start(out=c_aggr_sb[c][:], in_=c_aggr_rows[:, c * CHUNK_TILES : (c + 1) * CHUNK_TILES, :])
+            first, tiles = FIRST_TILE[c], CHUNK_LIST[c]
+            c_aggr_sb[c] = loads.tile([P, tiles, H_DIM], BF16, name="c_aggr_sb")
+            nc.sync.dma_start(out=c_aggr_sb[c][:], in_=c_aggr_rows[:, first : first + tiles, :])
 
         def mask_x(c):
-            if XMODE == "sdiag" or c in XSTRIDED:
-                diag[c] = ordered.tile([P, CHUNK_TILES, P], F32, name="diag")
-                for j in range(CHUNK_TILES):
-                    t = c * CHUNK_TILES + j
-                    nc.scalar.activation(out=diag[c][:, j, :], in_=ident[:], func=ACT.Copy, scale=mask_f32[:, t : t + 1])
-                return
-            if XMODE == "diag":
-                diag[c] = ordered.tile([P, CHUNK_TILES, P], F32, name="diag")
+            diag[c] = ordered.tile([P, CHUNK_TILES, P], F32, name="diag", bufs=3)
+            first, tiles = FIRST_TILE[c], CHUNK_LIST[c]
+            if XMODE == "sdiag" or c < 3:
+                for j in range(tiles):
+                    nc.scalar.activation(
+                        out=diag[c][:, j, :], in_=ident[:], func=ACT.Copy, scale=mask_f32[:, first + j : first + j + 1]
+                    )
+            elif XMODE == "gts":
+                for j in range(tiles):
+                    nc.gpsimd.tensor_scalar(
+                        out=diag[c][:, j, :],
+                        in0=ident[:],
+                        scalar1=mask_f32[:, first + j : first + j + 1],
+                        scalar2=0.0,
+                        op0=ALU.mult,
+                        op1=ALU.add,
+                    )
+            elif XMODE == "vts":
+                for j in range(tiles):
+                    nc.vector.tensor_scalar(
+                        out=diag[c][:, j, :],
+                        in0=ident[:],
+                        scalar1=mask_f32[:, first + j : first + j + 1],
+                        scalar2=None,
+                        op0=ALU.mult,
+                    )
+            else:
                 nc.gpsimd.tensor_tensor(
-                    out=diag[c][:],
-                    in0=ident[:].unsqueeze(1).to_broadcast([P, CHUNK_TILES, P]),
-                    in1=mask_col[:, c * CHUNK_TILES : (c + 1) * CHUNK_TILES].unsqueeze(2).to_broadcast([P, CHUNK_TILES, P]),
+                    out=diag[c][:, 0:tiles, :],
+                    in0=ident[:].unsqueeze(1).to_broadcast([P, tiles, P]),
+                    in1=mask_col[:, first : first + tiles].unsqueeze(2).to_broadcast([P, tiles, P]),
                     op=ALU.mult,
-                )
-                return
-            x_ordered[c] = ordered.tile([P, CHUNK_TILES, 2, WORDS, 2], BF16, name="x_ordered", bufs=3)
-            for j in range(CHUNK_TILES):
-                t = c * CHUNK_TILES + j
-                eng = nc.gpsimd if XMODE == "g" else nc.vector
-                eng.tensor_scalar(
-                    out=x_ordered[c][:, j, :, :, :],
-                    in0=x_sb[c][:, j * X_DIM : (j + 1) * X_DIM].rearrange("p (w u e) -> p u w e", u=2, e=2),
-                    scalar1=mask_f32[:, t : t + 1],
-                    scalar2=0.0,
-                    op0=ALU.mult,
-                    op1=ALU.add,
                 )
 
         def order_hf(c, g):
             if (c, g) in HSTRIDED:
                 return
             if c not in hf_ordered:
-                hf_ordered[c] = ordered.tile([P, PASSES - 1, CHUNK_TILES, 2, WORDS], F32, name="hf_ordered")
+                hf_ordered[c] = ordered.tile([P, PASSES - 1, CHUNK_LIST[c], 2, WORDS], F32, name="hf_ordered")
             words = hf_sb[c][:].bitcast(F32).rearrange("p (j h w u) -> p h j u w", h=PASSES - 1, w=WORDS, u=2)
             nc.vector.tensor_copy(out=hf_ordered[c][:, g - 1, :, :, :], in_=words[:, g - 1, :, :, :])
 
@@ -131,10 +145,21 @@ def tile_treelstmcell_pb_t_kernel(
             spread = psum.tile([P, SPREAD_TILES, P], BF16, name="spread", tag="bank")
             for j in range(SPREAD_TILES):
                 t = first_tile + j
-                nc.tensor.transpose(spread[:, j, :], mask_col[:, t : t + 1].to_broadcast([P, P]), ident_bf[:])
+                nc.tensor.matmul(
+                    out=spread[:, j, :],
+                    lhsT=mask_col[:, t : t + 1].to_broadcast([P, P]),
+                    rhs=ident_bf[:],
+                    start=True,
+                    stop=True,
+                )
             nc.scalar.copy(out=mask_row[:, first_tile : first_tile + SPREAD_TILES, :], in_=spread[:])
 
-        def transpose_in(c, g):
+        def keep_busy(count):
+            for i in range(count):
+                idle = psum.tile([P, CHUNK], F32, name="idle", tag="bank")
+                nc.tensor.matmul(out=idle[:], lhsT=ident_bf[:], rhs=zeros[:], start=True, stop=True)
+
+        def transpose_in(c, g, halves=None):
             if c not in a_grouped:
                 a_grouped[c] = acts.tile([P, PASSES * CHUNK * PACK], BF16, name="a_grouped", align_bytes=64)
             perm = lambda j: ident[:]
@@ -142,9 +167,6 @@ def tile_treelstmcell_pb_t_kernel(
                 sw = x_sb[c][:].bitcast(F32)
                 words = lambda j, u: sw[:, j * (X_DIM // 2) + u : (j + 1) * (X_DIM // 2) : 2]
                 perm = lambda j: diag[c][:, j, :]
-            elif g == 0:
-                x_words = x_ordered[c][:].rearrange("p j u w e -> p (j u w e)").bitcast(F32)
-                words = lambda j, u: x_words[:, (2 * j + u) * WORDS : (2 * j + u + 1) * WORDS]
             elif (c, g) not in HSTRIDED:
                 words = lambda j, u: hf_ordered[c][:, g - 1, j, u, :]
             else:
@@ -154,7 +176,7 @@ def tile_treelstmcell_pb_t_kernel(
                     :, j * (HF_DIM // 2) + first_word + u : j * (HF_DIM // 2) + first_word + K_PASS // 2 : 2
                 ]
             grouped_words = a_grouped[c][:].bitcast(F32)
-            for half in range(HALVES):
+            for half in (halves or range(CHUNK_LIST[c] // BANK_TILES)):
                 kT = psum.tile([P, 2, BANK_TILES * P], F32, name="kT", tag="bank")
                 for jj in range(BANK_TILES):
                     j = half * BANK_TILES + jj
@@ -170,25 +192,25 @@ def tile_treelstmcell_pb_t_kernel(
             if c not in a_codes:
                 a_codes[c] = acts.tile([P, PASSES * CHUNK], U32, name="a_codes", align_bytes=64)
                 a_scales[c] = acts.tile([P, PASSES * CHUNK], U8, name="a_scales", align_bytes=64)
-            cols = slice(g * CHUNK, (g + 1) * CHUNK)
+            first, nodes = g * CHUNK, CHUNK_LIST[c] * P
             nc.vector.quantize_mx(
-                out=a_codes[c][:, cols].bitcast(FP8X4),
-                scales=a_scales[c][:, cols],
-                in_=a_grouped[c][:, g * CHUNK * PACK : (g + 1) * CHUNK * PACK],
+                out=a_codes[c][:, first : first + nodes].bitcast(FP8X4),
+                scales=a_scales[c][:, first : first + nodes],
+                in_=a_grouped[c][:, first * PACK : (first + nodes) * PACK],
             )
 
         def gate_sums(c, some, pass_by_pass=False):
             if c not in gates:
                 gates[c] = work.tile([P, GATE_TILES, CHUNK], F32, name="gates")
             for m in some:
-                sums[m] = psum.tile([P, CHUNK], F32, name="sums", tag="bank")
+                sums[m] = psum.tile([P, CHUNK_LIST[c] * P], F32, name="sums", tag="bank")
             if pass_by_pass:
                 order = [(m, g) for g in range(PASSES) for m in some]
             else:
                 order = [(m, g) for m in some for g in range(PASSES)]
             for m, g in order:
                 w_cols = slice(g * GATES + m * P, g * GATES + (m + 1) * P)
-                a_cols = slice(g * CHUNK, (g + 1) * CHUNK)
+                a_cols = slice(g * CHUNK, g * CHUNK + CHUNK_LIST[c] * P)
                 nc.tensor.matmul_mx(
                     out=sums[m][:],
                     lhsT=w_codes[:, w_cols].bitcast(FP8X4),
@@ -200,17 +222,18 @@ def tile_treelstmcell_pb_t_kernel(
                 )
         def gate_exits(c, some):
             for m in some:
-                masked = work.tile([P, CHUNK], F32, name="masked", bufs=4)
+                first, tiles = FIRST_TILE[c], CHUNK_LIST[c]
+                masked = work.tile([P, tiles * P], F32, name="masked", bufs=4)
                 nc.vector.scalar_tensor_tensor(
                     out=masked[:],
-                    in0=mask_row[:, c * CHUNK_TILES : (c + 1) * CHUNK_TILES, :].rearrange("q t p -> q (t p)"),
+                    in0=mask_row[:, first : first + tiles, :].rearrange("q t p -> q (t p)"),
                     scalar=bias_col[:, m : m + 1],
                     in1=sums[m][:],
                     op0=ALU.mult,
                     op1=ALU.add,
                 )
                 nc.scalar.activation(
-                    out=gates[c][:, m, :],
+                    out=gates[c][:, m, 0 : tiles * P],
                     in_=masked[:],
                     func=(ACT.Tanh if m in U_TILES else ACT.Sigmoid),
                     bias=bias_col[:, GATE_TILES + m : GATE_TILES + m + 1],
@@ -223,8 +246,9 @@ def tile_treelstmcell_pb_t_kernel(
 
         def multiply_i_u(c):
             i_times_u[c] = work.tile([P, H_TILES, CHUNK], F32, name="i_times_u")
-            for half in range(HALVES):
-                cols = slice(half * BANK_TILES * P, (half + 1) * BANK_TILES * P)
+            width = CHUNK_LIST[c] * P // IU_PIECES
+            for piece in range(IU_PIECES):
+                cols = slice(piece * width, (piece + 1) * width)
                 nc.gpsimd.tensor_tensor(
                     out=i_times_u[c][:, :, cols],
                     in0=gates[c][:, I_TILES[0] : I_TILES[0] + H_TILES, cols],
@@ -242,24 +266,27 @@ def tile_treelstmcell_pb_t_kernel(
                     )
             return back
 
-        def cell_state(c):
-            c_new[c] = work.tile([P, CHUNK_TILES, H_DIM], F32, name="c_new")
-            tanh_c[c] = work.tile([P, CHUNK_TILES, H_DIM], F32, name="tanh_c")
-            for half in range(HALVES):
+        def cell_state(c, halves=None):
+            if c not in c_new:
+                c_new[c] = work.tile([P, CHUNK_TILES, H_DIM], F32, name="c_new")
+                tanh_c[c] = work.tile([P, CHUNK_TILES, H_DIM], F32, name="tanh_c")
+            for half in (halves or range(CHUNK_LIST[c] // BANK_TILES)):
                 tiles = slice(half * BANK_TILES, (half + 1) * BANK_TILES)
                 back = transpose_back(i_times_u[c], 0, half)
                 nc.vector.tensor_tensor(out=c_new[c][:, tiles, :], in0=back[:], in1=c_aggr_sb[c][:, tiles, :], op=ALU.add)
                 nc.scalar.activation(out=tanh_c[c][:, tiles, :], in_=c_new[c][:, tiles, :], func=ACT.Tanh)
-                first = c * CHUNK_TILES + half * BANK_TILES
+                first = FIRST_TILE[c] + half * BANK_TILES
                 nc.sync.dma_start(out=c_rows[:, first : first + BANK_TILES, :], in_=c_new[c][:, tiles, :])
 
-        def hidden_state(c):
-            h_new = work.tile([P, CHUNK_TILES, H_DIM], F32, name="h_new")
-            for half in range(HALVES):
+        def hidden_state(c, halves=None):
+            if c not in h_state:
+                h_state[c] = work.tile([P, CHUNK_TILES, H_DIM], F32, name="h_new")
+            h_new = h_state[c]
+            for half in (halves or range(CHUNK_LIST[c] // BANK_TILES)):
                 tiles = slice(half * BANK_TILES, (half + 1) * BANK_TILES)
                 back = transpose_back(gates[c], O_TILES[0], half)
                 nc.vector.tensor_tensor(out=h_new[:, tiles, :], in0=back[:], in1=tanh_c[c][:, tiles, :], op=ALU.mult)
-                first = c * CHUNK_TILES + half * BANK_TILES
+                first = FIRST_TILE[c] + half * BANK_TILES
                 nc.sync.dma_start(out=h_rows[:, first : first + BANK_TILES, :], in_=h_new[:, tiles, :])
 
         w_codes = const.tile([P, PASSES * GATES], U32, align_bytes=64)
@@ -294,60 +321,59 @@ def tile_treelstmcell_pb_t_kernel(
 
         bias_rows = const.tile([P, P], BF16)
         nc.vector.memset(bias_rows[:], 0.0)
+        zeros = const.tile([P, CHUNK], BF16)
+        nc.vector.memset(zeros[:], 0.0)
         warm = const.tile([P, 1], BF16)
         nc.scalar.activation(out=warm[:], in_=bias_rows[:, 0:1], func=ACT.Sigmoid)
         nc.vector.tensor_copy(out=mask_f32[:], in_=mask_col[:])
-        load_weights(0, I_PART)
+        load_weights(0, (0, GATES))
+        load_weights(1, (0, GATES))
         load_x(0)
-        load_weights(1, I_PART)
-        load_hf(0)
+        load_weights(2, (0, GATES))
         nc.sync.dma_start(out=bias_rows[0:GATE_TILES, :], in_=b_iou_in.rearrange("(m g) -> m g", g=P))
         nc.sync.dma_start(out=bias_rows[GATE_TILES : 2 * GATE_TILES, :], in_=b_aggr_iou.rearrange("(m g) -> m g", g=P))
-        load_weights(2, I_PART)
-        for g in range(PASSES):
-            load_weights(g, OU_PART)
+        load_hf(0)
         load_x(1)
         load_hf(1)
         load_c_aggr(0)
         load_x(2)
         load_hf(2)
-        mask_x(0)
-        mask_x(1)
-        for t in range(0, NODE_TILES, SPREAD_TILES):
+        for i, t in enumerate(range(0, NODE_TILES, SPREAD_TILES)):
             spread_mask(t)
-        group_weights(0, I_PART)
+            if i < 3:
+                mask_x(i)
+        keep_busy(4)
+        for g in range(2):
+            group_weights(g, I_PART)
+            group_weights(g, U_PART)
+            quantise_weights(g, I_PART)
+            quantise_weights(g, U_PART)
         transpose_in(0, 0)
-        group_weights(1, I_PART)
-        quantise_weights(0, I_PART)
+        keep_busy(3)
         quantise(0, 0)
-        quantise_weights(1, I_PART)
-        transpose_in(0, 1)
-        transpose_in(0, 2)
+        group_weights(2, I_PART)
+        group_weights(2, U_PART)
+        quantise_weights(2, I_PART)
+        quantise_weights(2, U_PART)
         bias_ps = psum.tile([P, P], BF16, name="bias_ps", tag="bank")
         nc.tensor.transpose(bias_ps[:], bias_rows[:], ident_bf[:])
         bias_col = const.tile([P, 2 * GATE_TILES], F32)
         nc.vector.tensor_copy(out=bias_col[:], in_=bias_ps[:, 0 : 2 * GATE_TILES])
-        group_weights(2, I_PART)
+        for half in range(CHUNK_LIST[0] // BANK_TILES):
+            transpose_in(0, 1, (half,))
+            transpose_in(0, 2, (half,))
+            keep_busy(1)
+        keep_busy(0)
         quantise(0, 1)
-        quantise_weights(2, I_PART)
         quantise(0, 2)
+        for g in range(PASSES):
+            group_weights(g, O_PART, True)
         gate_sums(0, I_TILES, True)
-        group_weights(0, O_PART, True)
-        group_weights(1, O_PART, True)
-        group_weights(2, O_PART, True)
-        group_weights(0, U_PART)
-        group_weights(1, U_PART)
-        quantise_weights(0, U_PART)
         gate_exits(0, I_TILES)
-        group_weights(2, U_PART)
-        quantise_weights(1, U_PART)
-        quantise_weights(2, U_PART)
+        for g in range(PASSES):
+            quantise_weights(g, O_PART)
         transpose_in(1, 0)
-        gate_sums(0, U_TILES)
-        quantise_weights(0, O_PART)
-        gate_exits(0, U_TILES)
-        quantise_weights(1, O_PART)
-        quantise_weights(2, O_PART)
+        gate_tiles(0, U_TILES)
         multiply_i_u(0)
         quantise(1, 0)
         transpose_in(1, 1)
@@ -358,34 +384,49 @@ def tile_treelstmcell_pb_t_kernel(
                 load_hf(c + 3)
             if c + 1 < CHUNKS:
                 load_c_aggr(c + 1)
-            if c + 2 < CHUNKS:
+            if 0 < c and c + 2 < CHUNKS:
                 mask_x(c + 2)
             if c + 2 < CHUNKS:
                 order_hf(c + 2, 1)
-
             if 0 < c and c + 1 < CHUNKS:
-                transpose_in(c + 1, 1)
+                transpose_in(c + 1, 1, (0,))
+            if 0 < c and c + 1 < CHUNKS:
+                transpose_in(c + 1, 1, (1,))
             if 0 < c < CHUNKS:
-                gate_tiles(c, I_TILES)
-
+                gate_tiles(c, (0,))
+            if 0 < c < CHUNKS:
+                gate_tiles(c, (1,))
             if 0 <= c - 1:
-                cell_state(c - 1)
+                cell_state(c - 1, (0,))
+            if 0 <= c - 1:
+                cell_state(c - 1, (1,))
             if c + 1 < CHUNKS:
-                transpose_in(c + 1, 2)
-                if c > 0:
-                    quantise(c + 1, 0)
+                transpose_in(c + 1, 2, (0,))
+            if c + 1 < CHUNKS:
+                transpose_in(c + 1, 2, (1,))
+            if 0 < c and c + 1 < CHUNKS:
+                quantise(c + 1, 0)
+            if c + 1 < CHUNKS:
                 quantise(c + 1, 1)
             if c + 2 < CHUNKS:
                 order_hf(c + 2, 2)
             if 0 < c < CHUNKS:
-                gate_tiles(c, U_TILES)
+                gate_tiles(c, (4,))
+            if 0 < c < CHUNKS:
+                gate_tiles(c, (5,))
+            if 0 < c < CHUNKS:
                 multiply_i_u(c)
             if c + 1 < CHUNKS:
                 quantise(c + 1, 2)
-
             if 0 <= c - 1:
-                hidden_state(c - 1)
+                hidden_state(c - 1, (0,))
+            if 0 <= c - 1:
+                hidden_state(c - 1, (1,))
             if c + 2 < CHUNKS:
-                transpose_in(c + 2, 0)
+                transpose_in(c + 2, 0, (0,))
+            if c + 2 < CHUNKS:
+                transpose_in(c + 2, 0, (1,))
             if c < CHUNKS:
-                gate_tiles(c, O_TILES)
+                gate_tiles(c, (2,))
+            if c < CHUNKS:
+                gate_tiles(c, (3,))

@@ -33,8 +33,7 @@ I_TILES, O_TILES, U_TILES = (0, 1), (2, 3), (4, 5)
 I_PART, O_PART, U_PART = (0, H_DIM), (H_DIM, H_DIM), (2 * H_DIM, H_DIM)
 OU_PART = (H_DIM, 2 * H_DIM)
 
-IU_PIECES = 2
-XMODE = "sdiag"
+XMODE = "gx"
 XSTRIDED = ()
 HSTRIDED = ((0, 1), (0, 2), (1, 1), (1, 2), (2, 1), (2, 2), (3, 1), (3, 2), (4, 1), (4, 2), (5, 1), (5, 2), (6, 1), (6, 2), (7, 1), (7, 2))
 FLOPS = 2 * NODES * (X_DIM + HF_DIM) * GATES
@@ -106,6 +105,17 @@ def tile_treelstmcell_pb_t_kernel(
                     nc.scalar.activation(
                         out=diag[c][:, j, :], in_=ident[:], func=ACT.Copy, scale=mask_f32[:, first + j : first + j + 1]
                     )
+            elif XMODE == "gx":
+                x_ordered[c] = ordered.tile([P, CHUNK_TILES, 2, WORDS, 2], BF16, name="x_ordered", bufs=3)
+                for j in range(tiles):
+                    nc.gpsimd.tensor_scalar(
+                        out=x_ordered[c][:, j, :, :, :],
+                        in0=x_sb[c][:, j * X_DIM : (j + 1) * X_DIM].rearrange("p (w u e) -> p u w e", u=2, e=2),
+                        scalar1=mask_f32[:, first + j : first + j + 1],
+                        scalar2=0.0,
+                        op0=ALU.mult,
+                        op1=ALU.add,
+                    )
             elif XMODE == "gts":
                 for j in range(tiles):
                     nc.gpsimd.tensor_scalar(
@@ -163,7 +173,10 @@ def tile_treelstmcell_pb_t_kernel(
             if c not in a_grouped:
                 a_grouped[c] = acts.tile([P, PASSES * CHUNK * PACK], BF16, name="a_grouped", align_bytes=64)
             perm = lambda j: ident[:]
-            if g == 0 and c in diag:
+            if g == 0 and c in x_ordered:
+                x_words = x_ordered[c][:].rearrange("p j u w e -> p (j u w e)").bitcast(F32)
+                words = lambda j, u: x_words[:, (2 * j + u) * WORDS : (2 * j + u + 1) * WORDS]
+            elif g == 0 and c in diag:
                 sw = x_sb[c][:].bitcast(F32)
                 words = lambda j, u: sw[:, j * (X_DIM // 2) + u : (j + 1) * (X_DIM // 2) : 2]
                 perm = lambda j: diag[c][:, j, :]
@@ -244,17 +257,16 @@ def tile_treelstmcell_pb_t_kernel(
             gate_sums(c, some, pass_by_pass)
             gate_exits(c, some)
 
-        def multiply_i_u(c):
-            i_times_u[c] = work.tile([P, H_TILES, CHUNK], F32, name="i_times_u")
-            width = CHUNK_LIST[c] * P // IU_PIECES
-            for piece in range(IU_PIECES):
-                cols = slice(piece * width, (piece + 1) * width)
-                nc.gpsimd.tensor_tensor(
-                    out=i_times_u[c][:, :, cols],
-                    in0=gates[c][:, I_TILES[0] : I_TILES[0] + H_TILES, cols],
-                    in1=gates[c][:, U_TILES[0] : U_TILES[0] + H_TILES, cols],
-                    op=ALU.mult,
-                )
+        def multiply_i_u(c, f, half, on_vector=False):
+            if c not in i_times_u:
+                i_times_u[c] = work.tile([P, H_TILES, CHUNK], F32, name="i_times_u")
+            cols = slice(half * BANK_TILES * P, (half + 1) * BANK_TILES * P)
+            (nc.vector if on_vector else nc.gpsimd).tensor_tensor(
+                out=i_times_u[c][:, f, cols],
+                in0=gates[c][:, I_TILES[f], cols],
+                in1=gates[c][:, U_TILES[f], cols],
+                op=ALU.mult,
+            )
 
         def transpose_back(source, first_tile, half):
             back = psum.tile([P, BANK_TILES, H_DIM], F32, name="back", tag="bank")
@@ -374,7 +386,9 @@ def tile_treelstmcell_pb_t_kernel(
             quantise_weights(g, O_PART)
         transpose_in(1, 0)
         gate_tiles(0, U_TILES)
-        multiply_i_u(0)
+        for f in range(H_TILES):
+            for half in range(CHUNK_LIST[0] // BANK_TILES):
+                multiply_i_u(0, f, half)
         quantise(1, 0)
         transpose_in(1, 1)
 
@@ -386,8 +400,6 @@ def tile_treelstmcell_pb_t_kernel(
                 load_c_aggr(c + 1)
             if 0 < c and c + 2 < CHUNKS:
                 mask_x(c + 2)
-            if c + 2 < CHUNKS:
-                order_hf(c + 2, 1)
             if 0 < c and c + 1 < CHUNKS:
                 transpose_in(c + 1, 1, (0,))
             if 0 < c and c + 1 < CHUNKS:
@@ -408,14 +420,18 @@ def tile_treelstmcell_pb_t_kernel(
                 quantise(c + 1, 0)
             if c + 1 < CHUNKS:
                 quantise(c + 1, 1)
-            if c + 2 < CHUNKS:
-                order_hf(c + 2, 2)
             if 0 < c < CHUNKS:
                 gate_tiles(c, (4,))
             if 0 < c < CHUNKS:
                 gate_tiles(c, (5,))
             if 0 < c < CHUNKS:
-                multiply_i_u(c)
+                multiply_i_u(c, 0, 0)
+            if 0 < c < CHUNKS:
+                multiply_i_u(c, 1, 0)
+            if 0 < c < CHUNKS:
+                multiply_i_u(c, 0, 1)
+            if 0 < c < CHUNKS:
+                multiply_i_u(c, 1, 1)
             if c + 1 < CHUNKS:
                 quantise(c + 1, 2)
             if 0 <= c - 1:

from contextlib import ExitStack

import concourse.mybir as mybir
from concourse.masks import make_identity

BF16 = mybir.dt.bfloat16
F32 = mybir.dt.float32
U32 = mybir.dt.uint32
U8 = mybir.dt.uint8
FP8X4 = mybir.dt.float8_e4m3fn_x4
ACT = mybir.ActivationFunctionType
ALU = mybir.AluOpType

P = 128
PACK = 4
K_PASS = P * PACK
NODES, X_DIM, CHILDREN, H_DIM = 4096, 512, 4, 256
HF_DIM = CHILDREN * H_DIM
GATES = 3 * H_DIM
PASSES = (X_DIM + HF_DIM) // K_PASS
GATE_TILES = GATES // P
H_TILES = H_DIM // P
NODE_TILES = NODES // P
CHUNK = 512
CHUNK_TILES = CHUNK // P
CHUNK_LIST = (4, 4, 4, 4, 4, 4, 4, 4)
CHUNKS = len(CHUNK_LIST)
FIRST_TILE = [sum(CHUNK_LIST[:c]) for c in range(CHUNKS)]
WORDS = P
BANK_TILES = 2
SPREAD_TILES = 8
I_TILES, O_TILES, U_TILES = (0, 1), (2, 3), (4, 5)
I_PART, O_PART, U_PART = (0, H_DIM), (H_DIM, H_DIM), (2 * H_DIM, H_DIM)
OU_PART = (H_DIM, 2 * H_DIM)

XMODE = "gx"
XSTRIDED = ()
HSTRIDED = ((0, 1), (0, 2), (1, 1), (1, 2), (2, 1), (2, 2), (3, 1), (3, 2), (4, 1), (4, 2), (5, 1), (5, 2), (6, 1), (6, 2), (7, 1), (7, 2))
FLOPS = 2 * NODES * (X_DIM + HF_DIM) * GATES


def tile_treelstmcell_pb_t_kernel(
    tc, x, x_mask, neighbour_h, c_aggr, W_iou_in, b_iou_in, W_aggr_iou, b_aggr_iou, out_0, out_1
):
    nc = tc.nc

    x_rows = x.rearrange("(p t) k -> p (t k)", t=NODE_TILES)
    hf_rows = neighbour_h.rearrange("(p t) c f -> p (t c f)", t=NODE_TILES)
    c_aggr_rows = c_aggr.rearrange("(p t) f -> p t f", t=NODE_TILES)
    h_rows = out_0.rearrange("(p t) f -> p t f", t=NODE_TILES)
    c_rows = out_1.rearrange("(p t) f -> p t f", t=NODE_TILES)

    with ExitStack() as ctx:
        const = ctx.enter_context(tc.tile_pool(name="const", bufs=1))
        wstage = ctx.enter_context(tc.tile_pool(name="wstage", bufs=3))
        loads = ctx.enter_context(tc.tile_pool(name="loads", bufs=3))
        ordered = ctx.enter_context(tc.tile_pool(name="ordered", bufs=2))
        acts = ctx.enter_context(tc.tile_pool(name="acts", bufs=2))
        work = ctx.enter_context(tc.tile_pool(name="work", bufs=2))
        psum = ctx.enter_context(tc.psum_pool(name="psum", bufs=8))

        ctx.enter_context(tc.manual_schedule())

        x_sb, hf_sb, c_aggr_sb = {}, {}, {}
        x_ordered, hf_ordered, diag = {}, {}, {}
        w_raw, w_grouped = {}, {}
        a_grouped, a_codes, a_scales = {}, {}, {}
        gates, sums, i_times_u, c_new, tanh_c, h_state = {}, {}, {}, {}, {}, {}

        ident = const.tile([P, P], F32)
        make_identity(nc, ident[:])
        ident_bf = const.tile([P, P], BF16)
        make_identity(nc, ident_bf[:])

        mask_col = const.tile([P, NODE_TILES], BF16)
        nc.sync.dma_start(out=mask_col[:], in_=x_mask.rearrange("(p t) -> p t", t=NODE_TILES))
        mask_f32 = const.tile([P, NODE_TILES], F32)
        mask_row = const.tile([P, NODE_TILES, P], BF16)

        def load_x(c):
            first, tiles = FIRST_TILE[c], CHUNK_LIST[c]
            x_sb[c] = loads.tile([P, tiles * X_DIM], BF16, name="x_sb", bufs=4)
            nc.sync.dma_start(out=x_sb[c][:], in_=x_rows[:, first * X_DIM : (first + tiles) * X_DIM])

        def load_hf(c):
            first, tiles = FIRST_TILE[c], CHUNK_LIST[c]
            hf_sb[c] = loads.tile([P, tiles * HF_DIM], BF16, name="hf_sb")
            step = BANK_TILES if c == 0 else tiles
            for j in range(0, tiles, step):
                nc.sync.dma_start(
                    out=hf_sb[c][:, j * HF_DIM : (j + step) * HF_DIM],
                    in_=hf_rows[:, (first + j) * HF_DIM : (first + j + step) * HF_DIM],
                )

        def load_c_aggr(c):
            first, tiles = FIRST_TILE[c], CHUNK_LIST[c]
            c_aggr_sb[c] = loads.tile([P, tiles, H_DIM], BF16, name="c_aggr_sb")
            nc.sync.dma_start(out=c_aggr_sb[c][:], in_=c_aggr_rows[:, first : first + tiles, :])

        def mask_x(c):
            diag[c] = ordered.tile([P, CHUNK_TILES, P], F32, name="diag", bufs=3)
            first, tiles = FIRST_TILE[c], CHUNK_LIST[c]
            if XMODE == "sdiag" or c < 3:
                for j in range(tiles):
                    nc.scalar.activation(
                        out=diag[c][:, j, :], in_=ident[:], func=ACT.Copy, scale=mask_f32[:, first + j : first + j + 1]
                    )
            elif XMODE == "gx":
                x_ordered[c] = ordered.tile([P, CHUNK_TILES, 2, WORDS, 2], BF16, name="x_ordered", bufs=3)
                for j in range(tiles):
                    nc.gpsimd.tensor_scalar(
                        out=x_ordered[c][:, j, :, :, :],
                        in0=x_sb[c][:, j * X_DIM : (j + 1) * X_DIM].rearrange("p (w u e) -> p u w e", u=2, e=2),
                        scalar1=mask_f32[:, first + j : first + j + 1],
                        scalar2=0.0,
                        op0=ALU.mult,
                        op1=ALU.add,
                    )
            elif XMODE == "gts":
                for j in range(tiles):
                    nc.gpsimd.tensor_scalar(
                        out=diag[c][:, j, :],
                        in0=ident[:],
                        scalar1=mask_f32[:, first + j : first + j + 1],
                        scalar2=0.0,
                        op0=ALU.mult,
                        op1=ALU.add,
                    )
            elif XMODE == "vts":
                for j in range(tiles):
                    nc.vector.tensor_scalar(
                        out=diag[c][:, j, :],
                        in0=ident[:],
                        scalar1=mask_f32[:, first + j : first + j + 1],
                        scalar2=None,
                        op0=ALU.mult,
                    )
            else:
                nc.gpsimd.tensor_tensor(
                    out=diag[c][:, 0:tiles, :],
                    in0=ident[:].unsqueeze(1).to_broadcast([P, tiles, P]),
                    in1=mask_col[:, first : first + tiles].unsqueeze(2).to_broadcast([P, tiles, P]),
                    op=ALU.mult,
                )

        def order_hf(c, g):
            if (c, g) in HSTRIDED:
                return
            if c not in hf_ordered:
                hf_ordered[c] = ordered.tile([P, PASSES - 1, CHUNK_LIST[c], 2, WORDS], F32, name="hf_ordered")
            words = hf_sb[c][:].bitcast(F32).rearrange("p (j h w u) -> p h j u w", h=PASSES - 1, w=WORDS, u=2)
            nc.vector.tensor_copy(out=hf_ordered[c][:, g - 1, :, :, :], in_=words[:, g - 1, :, :, :])

        def spread_mask(first_tile):
            spread = psum.tile([P, SPREAD_TILES, P], BF16, name="spread", tag="bank")
            for j in range(SPREAD_TILES):
                t = first_tile + j
                nc.tensor.matmul(
                    out=spread[:, j, :],
                    lhsT=mask_col[:, t : t + 1].to_broadcast([P, P]),
                    rhs=ident_bf[:],
                    start=True,
                    stop=True,
                )
            nc.scalar.copy(out=mask_row[:, first_tile : first_tile + SPREAD_TILES, :], in_=spread[:])

        def keep_busy(count):
            for i in range(count):
                idle = psum.tile([P, CHUNK], F32, name="idle", tag="bank")
                nc.tensor.matmul(out=idle[:], lhsT=ident_bf[:], rhs=zeros[:], start=True, stop=True)

        def transpose_in(c, g, halves=None):
            if c not in a_grouped:
                a_grouped[c] = acts.tile([P, PASSES * CHUNK * PACK], BF16, name="a_grouped", align_bytes=64)
            perm = lambda j: ident[:]
            if g == 0 and c in x_ordered:
                x_words = x_ordered[c][:].rearrange("p j u w e -> p (j u w e)").bitcast(F32)
                words = lambda j, u: x_words[:, (2 * j + u) * WORDS : (2 * j + u + 1) * WORDS]
            elif g == 0 and c in diag:
                sw = x_sb[c][:].bitcast(F32)
                words = lambda j, u: sw[:, j * (X_DIM // 2) + u : (j + 1) * (X_DIM // 2) : 2]
                perm = lambda j: diag[c][:, j, :]
            elif (c, g) not in HSTRIDED:
                words = lambda j, u: hf_ordered[c][:, g - 1, j, u, :]
            else:
                hf_words = hf_sb[c][:].bitcast(F32)
                first_word = (g - 1) * (K_PASS // 2)
                words = lambda j, u: hf_words[
                    :, j * (HF_DIM // 2) + first_word + u : j * (HF_DIM // 2) + first_word + K_PASS // 2 : 2
                ]
            grouped_words = a_grouped[c][:].bitcast(F32)
            for half in (halves or range(CHUNK_LIST[c] // BANK_TILES)):
                kT = psum.tile([P, 2, BANK_TILES * P], F32, name="kT", tag="bank")
                for jj in range(BANK_TILES):
                    j = half * BANK_TILES + jj
                    for u in range(2):
                        nc.tensor.transpose(kT[:, u, jj * P : (jj + 1) * P], words(j, u), perm(j))
                first = (g * CHUNK + half * BANK_TILES * P) * 2
                nc.scalar.copy(
                    out=grouped_words[:, first : first + BANK_TILES * P * 2].rearrange("p (n u) -> p n u", u=2),
                    in_=kT[:].rearrange("p u n -> p n u"),
                )

        def quantise(c, g):
            if c not in a_codes:
                a_codes[c] = acts.tile([P, PASSES * CHUNK], U32, name="a_codes", align_bytes=64)
                a_scales[c] = acts.tile([P, PASSES * CHUNK], U8, name="a_scales", align_bytes=64)
            first, nodes = g * CHUNK, CHUNK_LIST[c] * P
            nc.vector.quantize_mx(
                out=a_codes[c][:, first : first + nodes].bitcast(FP8X4),
                scales=a_scales[c][:, first : first + nodes],
                in_=a_grouped[c][:, first * PACK : (first + nodes) * PACK],
            )

        def gate_sums(c, some, pass_by_pass=False):
            if c not in gates:
                gates[c] = work.tile([P, GATE_TILES, CHUNK], F32, name="gates")
            for m in some:
                sums[m] = psum.tile([P, CHUNK_LIST[c] * P], F32, name="sums", tag="bank")
            if pass_by_pass:
                order = [(m, g) for g in range(PASSES) for m in some]
            else:
                order = [(m, g) for m in some for g in range(PASSES)]
            for m, g in order:
                w_cols = slice(g * GATES + m * P, g * GATES + (m + 1) * P)
                a_cols = slice(g * CHUNK, g * CHUNK + CHUNK_LIST[c] * P)
                nc.tensor.matmul_mx(
                    out=sums[m][:],
                    lhsT=w_codes[:, w_cols].bitcast(FP8X4),
                    lhsT_scale=w_scales[:, w_cols],
                    rhs=a_codes[c][:, a_cols].bitcast(FP8X4),
                    rhs_scale=a_scales[c][:, a_cols],
                    start=(g == 0),
                    stop=(g == PASSES - 1),
                )
        def gate_exits(c, some):
            for m in some:
                first, tiles = FIRST_TILE[c], CHUNK_LIST[c]
                masked = work.tile([P, tiles * P], F32, name="masked", bufs=4)
                nc.vector.scalar_tensor_tensor(
                    out=masked[:],
                    in0=mask_row[:, first : first + tiles, :].rearrange("q t p -> q (t p)"),
                    scalar=bias_col[:, m : m + 1],
                    in1=sums[m][:],
                    op0=ALU.mult,
                    op1=ALU.add,
                )
                nc.scalar.activation(
                    out=gates[c][:, m, 0 : tiles * P],
                    in_=masked[:],
                    func=(ACT.Tanh if m in U_TILES else ACT.Sigmoid),
                    bias=bias_col[:, GATE_TILES + m : GATE_TILES + m + 1],
                    scale=1.0,
                )

        def gate_tiles(c, some, pass_by_pass=False):
            gate_sums(c, some, pass_by_pass)
            gate_exits(c, some)

        def multiply_i_u(c, f, half, on_vector=False):
            if c not in i_times_u:
                i_times_u[c] = work.tile([P, H_TILES, CHUNK], F32, name="i_times_u")
            cols = slice(half * BANK_TILES * P, (half + 1) * BANK_TILES * P)
            (nc.vector if on_vector else nc.gpsimd).tensor_tensor(
                out=i_times_u[c][:, f, cols],
                in0=gates[c][:, I_TILES[f], cols],
                in1=gates[c][:, U_TILES[f], cols],
                op=ALU.mult,
            )

        def transpose_back(source, first_tile, half):
            back = psum.tile([P, BANK_TILES, H_DIM], F32, name="back", tag="bank")
            for jj in range(BANK_TILES):
                j = half * BANK_TILES + jj
                for f in range(H_TILES):
                    nc.tensor.transpose(
                        back[:, jj, f * P : (f + 1) * P], source[:, first_tile + f, j * P : (j + 1) * P], ident[:]
                    )
            return back

        def cell_state(c, halves=None):
            if c not in c_new:
                c_new[c] = work.tile([P, CHUNK_TILES, H_DIM], F32, name="c_new")
                tanh_c[c] = work.tile([P, CHUNK_TILES, H_DIM], F32, name="tanh_c")
            for half in (halves or range(CHUNK_LIST[c] // BANK_TILES)):
                tiles = slice(half * BANK_TILES, (half + 1) * BANK_TILES)
                back = transpose_back(i_times_u[c], 0, half)
                nc.vector.tensor_tensor(out=c_new[c][:, tiles, :], in0=back[:], in1=c_aggr_sb[c][:, tiles, :], op=ALU.add)
                nc.scalar.activation(out=tanh_c[c][:, tiles, :], in_=c_new[c][:, tiles, :], func=ACT.Tanh)
                first = FIRST_TILE[c] + half * BANK_TILES
                nc.sync.dma_start(out=c_rows[:, first : first + BANK_TILES, :], in_=c_new[c][:, tiles, :])

        def hidden_state(c, halves=None):
            if c not in h_state:
                h_state[c] = work.tile([P, CHUNK_TILES, H_DIM], F32, name="h_new")
            h_new = h_state[c]
            for half in (halves or range(CHUNK_LIST[c] // BANK_TILES)):
                tiles = slice(half * BANK_TILES, (half + 1) * BANK_TILES)
                back = transpose_back(gates[c], O_TILES[0], half)
                nc.vector.tensor_tensor(out=h_new[:, tiles, :], in0=back[:], in1=tanh_c[c][:, tiles, :], op=ALU.mult)
                first = FIRST_TILE[c] + half * BANK_TILES
                nc.sync.dma_start(out=h_rows[:, first : first + BANK_TILES, :], in_=h_new[:, tiles, :])

        w_codes = const.tile([P, PASSES * GATES], U32, align_bytes=64)
        w_scales = const.tile([P, PASSES * GATES], U8, align_bytes=64)

        def load_weights(g, part):
            rows = W_iou_in if g == 0 else W_aggr_iou[(g - 1) * K_PASS : g * K_PASS, :]
            if g not in w_raw:
                w_raw[g] = wstage.tile([P, PACK, GATES], BF16, name="w_raw")
            first, cols = part
            nc.sync.dma_start(
                out=w_raw[g][:, :, first : first + cols],
                in_=rows[:, first : first + cols].rearrange("(q t) c -> q t c", t=PACK),
            )

        def group_weights(g, part, scalar=False):
            if g not in w_grouped:
                w_grouped[g] = wstage.tile([P, GATES, PACK], BF16, name="w_grouped", align_bytes=64)
            first, cols = part
            (nc.scalar.copy if scalar else nc.vector.tensor_copy)(
                out=w_grouped[g][:, first : first + cols, :],
                in_=w_raw[g][:, :, first : first + cols].rearrange("q t c -> q c t"),
            )

        def quantise_weights(g, part):
            first, cols = part
            nc.vector.quantize_mx(
                out=w_codes[:, g * GATES + first : g * GATES + first + cols].bitcast(FP8X4),
                scales=w_scales[:, g * GATES + first : g * GATES + first + cols],
                in_=w_grouped[g][:].rearrange("q c t -> q (c t)")[:, first * PACK : (first + cols) * PACK],
            )

        bias_rows = const.tile([P, P], BF16)
        nc.vector.memset(bias_rows[:], 0.0)
        zeros = const.tile([P, CHUNK], BF16)
        nc.vector.memset(zeros[:], 0.0)
        warm = const.tile([P, 1], BF16)
        nc.scalar.activation(out=warm[:], in_=bias_rows[:, 0:1], func=ACT.Sigmoid)
        nc.vector.tensor_copy(out=mask_f32[:], in_=mask_col[:])
        load_weights(0, (0, GATES))
        load_weights(1, (0, GATES))
        load_x(0)
        load_weights(2, (0, GATES))
        nc.sync.dma_start(out=bias_rows[0:GATE_TILES, :], in_=b_iou_in.rearrange("(m g) -> m g", g=P))
        nc.sync.dma_start(out=bias_rows[GATE_TILES : 2 * GATE_TILES, :], in_=b_aggr_iou.rearrange("(m g) -> m g", g=P))
        load_hf(0)
        load_x(1)
        load_hf(1)
        load_c_aggr(0)
        load_x(2)
        load_hf(2)
        for i, t in enumerate(range(0, NODE_TILES, SPREAD_TILES)):
            spread_mask(t)
            if i < 3:
                mask_x(i)
        keep_busy(4)
        for g in range(2):
            group_weights(g, I_PART)
            group_weights(g, U_PART)
            quantise_weights(g, I_PART)
            quantise_weights(g, U_PART)
        transpose_in(0, 0)
        keep_busy(3)
        quantise(0, 0)
        group_weights(2, I_PART)
        group_weights(2, U_PART)
        quantise_weights(2, I_PART)
        quantise_weights(2, U_PART)
        bias_ps = psum.tile([P, P], BF16, name="bias_ps", tag="bank")
        nc.tensor.transpose(bias_ps[:], bias_rows[:], ident_bf[:])
        bias_col = const.tile([P, 2 * GATE_TILES], F32)
        nc.vector.tensor_copy(out=bias_col[:], in_=bias_ps[:, 0 : 2 * GATE_TILES])
        for half in range(CHUNK_LIST[0] // BANK_TILES):
            transpose_in(0, 1, (half,))
            transpose_in(0, 2, (half,))
            keep_busy(1)
        keep_busy(0)
        quantise(0, 1)
        quantise(0, 2)
        for g in range(PASSES):
            group_weights(g, O_PART, True)
        gate_sums(0, I_TILES, True)
        gate_exits(0, I_TILES)
        for g in range(PASSES):
            quantise_weights(g, O_PART)
        transpose_in(1, 0)
        gate_tiles(0, U_TILES)
        for f in range(H_TILES):
            for half in range(CHUNK_LIST[0] // BANK_TILES):
                multiply_i_u(0, f, half)
        quantise(1, 0)
        transpose_in(1, 1)

        for c in range(CHUNKS + 1):
            if c + 3 < CHUNKS:
                load_x(c + 3)
                load_hf(c + 3)
            if c + 1 < CHUNKS:
                load_c_aggr(c + 1)
            if 0 < c and c + 2 < CHUNKS:
                mask_x(c + 2)
            if 0 < c and c + 1 < CHUNKS:
                transpose_in(c + 1, 1, (0,))
            if 0 < c and c + 1 < CHUNKS:
                transpose_in(c + 1, 1, (1,))
            if 0 < c < CHUNKS:
                gate_tiles(c, (0,))
            if 0 < c < CHUNKS:
                gate_tiles(c, (1,))
            if 0 <= c - 1:
                cell_state(c - 1, (0,))
            if 0 <= c - 1:
                cell_state(c - 1, (1,))
            if c + 1 < CHUNKS:
                transpose_in(c + 1, 2, (0,))
            if c + 1 < CHUNKS:
                transpose_in(c + 1, 2, (1,))
            if 0 < c and c + 1 < CHUNKS:
                quantise(c + 1, 0)
            if c + 1 < CHUNKS:
                quantise(c + 1, 1)
            if 0 < c < CHUNKS:
                gate_tiles(c, (4,))
            if 0 < c < CHUNKS:
                gate_tiles(c, (5,))
            if 0 < c < CHUNKS:
                multiply_i_u(c, 0, 0)
            if 0 < c < CHUNKS:
                multiply_i_u(c, 1, 0)
            if 0 < c < CHUNKS:
                multiply_i_u(c, 0, 1)
            if 0 < c < CHUNKS:
                multiply_i_u(c, 1, 1)
            if c + 1 < CHUNKS:
                quantise(c + 1, 2)
            if 0 <= c - 1:
                hidden_state(c - 1, (0,))
            if 0 <= c - 1:
                hidden_state(c - 1, (1,))
            if c + 2 < CHUNKS:
                transpose_in(c + 2, 0, (0,))
            if c + 2 < CHUNKS:
                transpose_in(c + 2, 0, (1,))
            if c < CHUNKS:
                gate_tiles(c, (2,))
            if c < CHUNKS:
                gate_tiles(c, (3,))
